import numpy as np
import ml_dtypes


def mxq(x, axis, fmt="e4m3"):
    dtype, down = {"e4m3": (ml_dtypes.float8_e4m3fn, 7), "e5m2": (ml_dtypes.float8_e5m2, 14)}[fmt]
    v = np.moveaxis(np.asarray(x, np.float32).astype(ml_dtypes.bfloat16).astype(np.float64), axis, -1)
    blocks = v.reshape(v.shape[:-1] + (-1, 32))
    amax = np.abs(blocks).max(-1, keepdims=True)
    byte = np.maximum(np.where(amax > 0, np.frexp(amax)[1] - 1 + 127, 0) - down, 1)
    scale = np.exp2(byte - 127.0)
    codes = (blocks / scale).astype(np.float32).astype(dtype).astype(np.float64)
    return np.moveaxis((codes * scale).reshape(v.shape), -1, axis)


WIDE = False


def mx_kscale(k):
    if not WIDE:
        return np.ones(k)
    levels = np.array([10, -10, 5, -5, 0])
    if k % 512:
        return np.exp2(np.random.permutation(np.resize(levels, k // 32))).repeat(32)
    a = np.empty((k // 512, 16))
    for p in range(k // 512):
        a[p, :8] = np.random.permutation(np.resize(levels, 8))
        for g in range(8):
            far = levels[np.abs(levels - a[p, g]) >= 10]
            a[p, g + 8] = far[np.random.randint(len(far))]
    return np.exp2(a.ravel()).repeat(32)


BF16 = ml_dtypes.bfloat16


def bf(x):
    return np.asarray(x, np.float32).astype(BF16)


def f64(x):
    return np.asarray(x).astype(np.float64)


B, IN, HID, BLK, OUT = 512, 1024, 4096, 512, 10
NB = HID // BLK


def setup_inputs():
    s = mx_kscale(IN)
    t = np.tile(mx_kscale(BLK), NB)
    return {
        "x": bf(np.random.standard_normal((B, IN)) * s),
        "W1": bf(np.random.standard_normal((HID, IN)) / np.sqrt(IN) / s * t[:, None]),
        "b1": bf(np.random.standard_normal(HID) * 0.3 * t),
        "Wb": bf(np.random.standard_normal((NB, BLK, BLK)) * 1.4 / np.sqrt(BLK) / t.reshape(NB, 1, BLK)),
        "bb": bf(np.random.standard_normal(HID) * 0.3),
    }


def reference(x, W1, b1, Wb, bb):
    h = np.maximum((mxq(f64(x), 1, "e4m3") @ mxq(f64(W1), 1, "e4m3").T) + f64(b1), 0.0)
    hb = h.reshape(B, NB, BLK)
    yb = (mxq(hb, 2, "e4m3").transpose(1, 0, 2) @ mxq(f64(Wb), 2, "e4m3").transpose(0, 2, 1)).transpose(1, 0, 2)
    return np.maximum(yb.reshape(B, HID) + f64(bb), 0.0)

@@ -1,0 +1,267 @@
+from contextlib import ExitStack
+
+import concourse.mybir as mybir
+from concourse.masks import make_identity
+
+F32 = mybir.dt.float32
+BF16 = mybir.dt.bfloat16
+U32 = mybir.dt.uint32
+U8 = mybir.dt.uint8
+FP8X4 = mybir.dt.float8_e4m3fn_x4
+RELU = mybir.ActivationFunctionType.Relu
+ADD = mybir.AluOpType.add
+
+P = 128
+BATCH = 512
+K1 = 1024
+HID = 4096
+CHUNK = 512
+N_CHUNKS = HID // CHUNK
+TILES = 4
+BANK = 512
+PSUM_BANKS = 8
+W1_AHEAD = 3
+WB_AHEAD = 2
+STAGE1_AHEAD = 2
+HELPED = 2
+SCALAR_RELU = (5, 6)
+
+FLOPS = 2 * BATCH * K1 * HID + 2 * BATCH * CHUNK * HID
+
+
+def tile_blockdiagmnistconvertible_pa_kernel(tc, x, W1, b1, Wb, bb, out):
+    nc = tc.nc
+    with ExitStack() as ctx:
+        const = ctx.enter_context(tc.tile_pool(name="const", bufs=1))
+        w1_pool = ctx.enter_context(tc.tile_pool(name="w1_pool", bufs=N_CHUNKS))
+        wb_pool = ctx.enter_context(tc.tile_pool(name="wb_pool", bufs=N_CHUNKS))
+        work = ctx.enter_context(tc.tile_pool(name="work", bufs=2))
+        slow = ctx.enter_context(tc.tile_pool(name="slow", bufs=3))
+        psum = ctx.enter_context(tc.psum_pool(name="psum", bufs=PSUM_BANKS))
+        ctx.enter_context(tc.manual_schedule())
+
+        ident = const.tile([P, P], F32)
+        make_identity(nc, ident[:])
+        b1_rows = const.tile([P, CHUNK], BF16)
+        nc.vector.memset(b1_rows[:], 0.0)
+        bb_rows = const.tile([P, CHUNK], BF16)
+        nc.vector.memset(bb_rows[:], 0.0)
+        nc.sync.dma_start(out=b1_rows[0:N_CHUNKS, :], in_=b1.rearrange("(n w) -> n w", w=CHUNK))
+        nc.sync.dma_start(out=bb_rows[0:N_CHUNKS, :], in_=bb.rearrange("(n o) -> n o", o=CHUNK))
+
+        x_sb = const.tile([P, TILES * K1], BF16)
+        x_src = x.rearrange("(c b) k -> c b k", b=TILES)
+        x_dst = x_sb[:].rearrange("c (b k) -> c b k", b=TILES)
+        for half in range(2):
+            nc.sync.dma_start(out=x_dst[:, 2 * half:2 * half + 2, :], in_=x_src[:, 2 * half:2 * half + 2, :])
+
+        w1_sb = {}
+        wb_sb = {}
+
+        def load_w1(n):
+            w1_tile = w1_pool.tile([P, TILES * K1], BF16)
+            w1_sb[n] = w1_tile
+            src = W1[n * CHUNK:(n + 1) * CHUNK, :].rearrange("(p t) k -> p t k", t=TILES)
+            dst = w1_tile[:].rearrange("p (t k) -> p t k", t=TILES)
+            if n == 0:
+                for half in range(2):
+                    nc.sync.dma_start(out=dst[:, 2 * half:2 * half + 2, :], in_=src[:, 2 * half:2 * half + 2, :])
+            else:
+                nc.sync.dma_start(out=dst, in_=src)
+
+        def load_wb(n):
+            wb_tile = wb_pool.tile([P, TILES * CHUNK], BF16)
+            wb_sb[n] = wb_tile
+            nc.sync.dma_start(out=wb_tile[:].rearrange("c (j k) -> c j k", j=TILES),
+                              in_=Wb[n].rearrange("(c j) k -> c j k", j=TILES))
+
+        load_w1(0)
+        for n in range(1, N_CHUNKS):
+            load_w1(n)
+            load_wb(n - 1)
+        load_wb(N_CHUNKS - 1)
+
+        ident_bf = const.tile([P, P], BF16)
+        nc.vector.tensor_copy(out=ident_bf[:], in_=ident[:])
+
+        def copy_out(on_vector, dst, src):
+            if on_vector:
+                nc.vector.tensor_copy(out=dst, in_=src)
+            else:
+                nc.scalar.copy(out=dst, in_=src)
+
+        def transpose_words(words, first):
+            bank = psum.tile([P, BANK], F32, tag="bank")
+            for i in range(4):
+                lo = first + 2 * P * (i // 2)
+                nc.tensor.transpose(out=bank[:, P * i:P * (i + 1)], in_=words[:, lo + i % 2:lo + 2 * P:2],
+                                    identity=ident[:])
+            return bank
+
+        b1_bank = psum.tile([P, BANK], F32, tag="bank")
+        for u in range(2):
+            nc.tensor.transpose(out=b1_bank[:, u * P:(u + 1) * P], in_=b1_rows[:].bitcast(F32)[:, u:2 * P:2],
+                                identity=ident[:])
+        b1_words = const.tile([P, 2 * N_CHUNKS], F32)
+        nc.vector.tensor_copy(out=b1_words[:].rearrange("p (n u) -> p n u", u=2),
+                              in_=b1_bank[:, 0:2 * P].rearrange("p (u r) -> p r u", u=2)[:, 0:N_CHUNKS, :])
+        b1_col = const.tile([P, TILES * N_CHUNKS], F32)
+        nc.vector.tensor_copy(out=b1_col[:], in_=b1_words[:].bitcast(BF16))
+
+        bb_all = const.tile([P, HID], BF16)
+
+        def spread_bb(n0, on_vector):
+            wide = psum.tile([P, 2 * CHUNK], BF16, tag="bank")
+            for s in range(2):
+                nc.tensor.matmul(out=wide[:, s * CHUNK:(s + 1) * CHUNK],
+                                 lhsT=ident_bf[:, n0 + s:n0 + s + 1].to_broadcast([P, P]),
+                                 rhs=bb_rows[:], start=True, stop=True)
+            copy_out(on_vector, bb_all[:, n0 * CHUNK:(n0 + 2) * CHUNK], wide[:])
+
+        spread_bb(0, True)
+        spread_bb(2, False)
+
+        x_grouped = const.tile([P, TILES * K1], BF16, align_bytes=64)
+        x_codes = const.tile([P, K1], U32, align_bytes=64)
+        x_scales = const.tile([P, K1], U8, align_bytes=64)
+        x_words = x_sb[:].bitcast(F32)
+        x_pairs = x_grouped[:].bitcast(F32).rearrange("p (g b c u) -> p g b c u", g=2, b=TILES, u=2)
+        for b in range(TILES):
+            bank = transpose_words(x_words, BANK * b)
+            copy_out(b % 2 == 1, x_pairs[:, :, b, :, :], bank[:].rearrange("p (g u c) -> p g c u", g=2, u=2))
+        for g in range(2):
+            nc.vector.quantize_mx(out=x_codes[:, g * BATCH:(g + 1) * BATCH].bitcast(FP8X4),
+                                  scales=x_scales[:, g * BATCH:(g + 1) * BATCH],
+                                  in_=x_grouped[:, g * TILES * BATCH:(g + 1) * TILES * BATCH])
+
+        w1_grouped = {}
+        w1_codes = {}
+        w1_scales = {}
+        wb_grouped = {}
+        wb_codes = {}
+        wb_scales = {}
+        h_planes = {}
+        h_grouped = {}
+        h_codes = {}
+        h_scales = {}
+        products = {}
+        out_sb = {}
+        out_rows = out.rearrange("(c b) o -> c b o", b=TILES)
+
+        def transpose_w1(n):
+            grouped = work.tile([P, TILES * K1], BF16, align_bytes=64, tag="w1_grouped")
+            w1_grouped[n] = grouped
+            words = w1_sb[n][:].bitcast(F32)
+            pairs = grouped[:].bitcast(F32)
+            for t in range(TILES):
+                bank = transpose_words(words, BANK * t)
+                copy_out(n < HELPED and t % 2 == 1,
+                         pairs[:, BANK * t:BANK * (t + 1)].rearrange("p (g c u) -> p g c u", g=2, u=2),
+                         bank[:].rearrange("p (g u c) -> p g c u", g=2, u=2))
+
+        def quantise_w1(n):
+            codes = work.tile([P, K1], U32, align_bytes=64, tag="w1_codes")
+            scales = work.tile([P, K1], U8, align_bytes=64, tag="w1_scales")
+            w1_codes[n] = codes
+            w1_scales[n] = scales
+            nc.vector.quantize_mx(out=codes[:].bitcast(FP8X4), scales=scales[:], in_=w1_grouped[n][:])
+
+        def transpose_wb(n):
+            grouped = work.tile([P, TILES * CHUNK], BF16, align_bytes=64, tag="wb_grouped")
+            wb_grouped[n] = grouped
+            words = wb_sb[n][:].bitcast(F32)
+            pairs = grouped[:].bitcast(F32).rearrange("p (c hi lu) -> p c hi lu", hi=2, lu=4)
+            for hi in range(2):
+                bank = transpose_words(words, BANK * hi)
+                copy_out(n < HELPED, pairs[:, :, hi, :], bank[:].rearrange("p (lu c) -> p c lu", lu=4))
+
+        def quantise_wb(n):
+            codes = slow.tile([P, CHUNK], U32, align_bytes=64, tag="wb_codes")
+            scales = slow.tile([P, CHUNK], U8, align_bytes=64, tag="wb_scales")
+            wb_codes[n] = codes
+            wb_scales[n] = scales
+            nc.vector.quantize_mx(out=codes[:].bitcast(FP8X4), scales=scales[:], in_=wb_grouped[n][:])
+
+        def stage1(n):
+            planes = work.tile([P, TILES * BATCH], BF16, tag="h_planes")
+            h_planes[n] = planes
+            for t in range(TILES):
+                acc = psum.tile([P, BATCH], F32, tag="bank")
+                for g in range(2):
+                    lo = (2 * t + g) * P
+                    nc.tensor.matmul_mx(out=acc[:], lhsT=w1_codes[n][:, lo:lo + P].bitcast(FP8X4),
+                                        lhsT_scale=w1_scales[n][:, lo:lo + P],
+                                        rhs=x_codes[:, g * BATCH:(g + 1) * BATCH].bitcast(FP8X4),
+                                        rhs_scale=x_scales[:, g * BATCH:(g + 1) * BATCH],
+                                        start=(g == 0), stop=(g == 1))
+                nc.scalar.activation(out=planes[:, t * BATCH:(t + 1) * BATCH], in_=acc[:], func=RELU,
+                                     bias=b1_col[:, TILES * n + t:TILES * n + t + 1], scale=1.0)
+
+        def regroup_h(n):
+            grouped = work.tile([P, TILES * BATCH], BF16, align_bytes=64, tag="h_grouped")
+            h_grouped[n] = grouped
+            nc.vector.tensor_copy(out=grouped[:].rearrange("p (run i t) -> p run t i", i=4, t=TILES),
+                                  in_=h_planes[n][:].rearrange("p (t run i) -> p run t i", t=TILES, i=4))
+
+        def quantise_h(n):
+            codes = work.tile([P, BATCH], U32, align_bytes=64, tag="h_codes")
+            scales = work.tile([P, BATCH], U8, align_bytes=64, tag="h_scales")
+            h_codes[n] = codes
+            h_scales[n] = scales
+            nc.vector.quantize_mx(out=codes[:].bitcast(FP8X4), scales=scales[:], in_=h_grouped[n][:])
+
+        def stage2(n):
+            for b in range(TILES):
+                acc = psum.tile([P, CHUNK], F32, tag="bank")
+                products[(n, b)] = acc
+                nc.tensor.matmul_mx(out=acc[:], lhsT=h_codes[n][:, b * P:(b + 1) * P].bitcast(FP8X4),
+                                    lhsT_scale=h_scales[n][:, b * P:(b + 1) * P],
+                                    rhs=wb_codes[n][:].bitcast(FP8X4), rhs_scale=wb_scales[n][:], start=True, stop=True)
+
+        def relu_and_store(n, first, last, on_vector):
+            part = out_sb[n][:, first * CHUNK:last * CHUNK]
+            if on_vector:
+                nc.vector.tensor_scalar_max(out=part, in0=part, scalar1=0.0)
+            else:
+                nc.scalar.activation(out=part, in_=part, func=RELU)
+            nc.sync.dma_start(out=out_rows[:, first:last, n * CHUNK:(n + 1) * CHUNK],
+                              in_=out_sb[n][:].rearrange("c (b o) -> c b o", b=TILES)[:, first:last, :])
+
+        def finish(n):
+            result = slow.tile([P, TILES * CHUNK], F32, tag="out_sb")
+            out_sb[n] = result
+            by_quarters = n in SCALAR_RELU or n == N_CHUNKS - 1
+            for b in range(TILES):
+                nc.vector.tensor_tensor(out=result[:, b * CHUNK:(b + 1) * CHUNK], in0=products[(n, b)][:],
+                                        in1=bb_all[:, n * CHUNK:(n + 1) * CHUNK], op=ADD)
+                if b == 1 and n + 1 < N_CHUNKS:
+                    quantise_h(n + 1)
+                if b == 0 or by_quarters:
+                    relu_and_store(n, b, b + 1, b > 0 and n not in SCALAR_RELU)
+            if not by_quarters:
+                relu_and_store(n, 1, TILES, True)
+
+        def exists(n):
+            return 0 <= n < N_CHUNKS
+
+        for p in range(-W1_AHEAD, N_CHUNKS):
+            if exists(p + W1_AHEAD):
+                transpose_w1(p + W1_AHEAD)
+            if exists(p + WB_AHEAD):
+                transpose_wb(p + WB_AHEAD)
+            if exists(p):
+                stage2(p)
+            if exists(p + STAGE1_AHEAD):
+                stage1(p + STAGE1_AHEAD)
+            if exists(p + 1):
+                regroup_h(p + 1)
+            if exists(p):
+                finish(p)
+            elif exists(p + 1):
+                quantise_h(p + 1)
+            if p in (1, 2):
+                spread_bb(2 * p + 2, False)
+            if exists(p + W1_AHEAD):
+                quantise_w1(p + W1_AHEAD)
+            if exists(p + WB_AHEAD):
+                quantise_wb(p + WB_AHEAD)

@@ -10,6 +10,8 @@ U8 = mybir.dt.uint8
 FP8X4 = mybir.dt.float8_e4m3fn_x4
 RELU = mybir.ActivationFunctionType.Relu
 ADD = mybir.AluOpType.add
+MAX = mybir.AluOpType.max
+MULT = mybir.AluOpType.mult
 
 P = 128
 BATCH = 512
@@ -20,11 +22,11 @@ N_CHUNKS = HID // CHUNK
 TILES = 4
 BANK = 512
 PSUM_BANKS = 8
-W1_AHEAD = 3
-WB_AHEAD = 2
-STAGE1_AHEAD = 2
-HELPED = 2
-SCALAR_RELU = (5, 6)
+W1_AHEAD = 2
+WB_AHEAD = 1
+STAGE1_AHEAD = 1
+HELPED = 1
+SCALAR_RELU = (5, 6, 7)
 
 FLOPS = 2 * BATCH * K1 * HID + 2 * BATCH * CHUNK * HID
 
@@ -155,7 +157,7 @@ def tile_blockdiagmnistconvertible_pa_kernel(tc, x, W1, b1, Wb, bb, out):
             pairs = grouped[:].bitcast(F32)
             for t in range(TILES):
                 bank = transpose_words(words, BANK * t)
-                copy_out(n < HELPED and t % 2 == 1,
+                copy_out(t == 3 or n < HELPED and t == 1,
                          pairs[:, BANK * t:BANK * (t + 1)].rearrange("p (g c u) -> p g c u", g=2, u=2),
                          bank[:].rearrange("p (g u c) -> p g c u", g=2, u=2))
 
@@ -218,50 +220,38 @@ def tile_blockdiagmnistconvertible_pa_kernel(tc, x, W1, b1, Wb, bb, out):
                                     lhsT_scale=h_scales[n][:, b * P:(b + 1) * P],
                                     rhs=wb_codes[n][:].bitcast(FP8X4), rhs_scale=wb_scales[n][:], start=True, stop=True)
 
-        def relu_and_store(n, first, last, on_vector):
-            part = out_sb[n][:, first * CHUNK:last * CHUNK]
-            if on_vector:
-                nc.vector.tensor_scalar_max(out=part, in0=part, scalar1=0.0)
-            else:
-                nc.scalar.activation(out=part, in_=part, func=RELU)
-            nc.sync.dma_start(out=out_rows[:, first:last, n * CHUNK:(n + 1) * CHUNK],
-                              in_=out_sb[n][:].rearrange("c (b o) -> c b o", b=TILES)[:, first:last, :])
-
         def finish(n):
             result = slow.tile([P, TILES * CHUNK], F32, tag="out_sb")
             out_sb[n] = result
-            by_quarters = n in SCALAR_RELU or n == N_CHUNKS - 1
             for b in range(TILES):
-                nc.vector.tensor_tensor(out=result[:, b * CHUNK:(b + 1) * CHUNK], in0=products[(n, b)][:],
+                part = result[:, b * CHUNK:(b + 1) * CHUNK]
+                nc.vector.tensor_tensor(out=part, in0=products[(n, b)][:],
                                         in1=bb_all[:, n * CHUNK:(n + 1) * CHUNK], op=ADD)
-                if b == 1 and n + 1 < N_CHUNKS:
-                    quantise_h(n + 1)
-                if b == 0 or by_quarters:
-                    relu_and_store(n, b, b + 1, b > 0 and n not in SCALAR_RELU)
-            if not by_quarters:
-                relu_and_store(n, 1, TILES, True)
+                if n in SCALAR_RELU:
+                    nc.scalar.activation(out=part, in_=part, func=RELU)
+                else:
+                    nc.gpsimd.tensor_scalar(out=part, in0=part, scalar1=0.0, scalar2=1.0, op0=MAX, op1=MULT)
+                nc.sync.dma_start(out=out_rows[:, b, n * CHUNK:(n + 1) * CHUNK], in_=part)
 
         def exists(n):
             return 0 <= n < N_CHUNKS
 
-        for p in range(-W1_AHEAD, N_CHUNKS):
-            if exists(p + W1_AHEAD):
-                transpose_w1(p + W1_AHEAD)
-            if exists(p + WB_AHEAD):
-                transpose_wb(p + WB_AHEAD)
-            if exists(p):
-                stage2(p)
-            if exists(p + STAGE1_AHEAD):
-                stage1(p + STAGE1_AHEAD)
-            if exists(p + 1):
-                regroup_h(p + 1)
-            if exists(p):
-                finish(p)
-            elif exists(p + 1):
-                quantise_h(p + 1)
-            if p in (1, 2):
-                spread_bb(2 * p + 2, False)
-            if exists(p + W1_AHEAD):
-                quantise_w1(p + W1_AHEAD)
-            if exists(p + WB_AHEAD):
-                quantise_wb(p + WB_AHEAD)
+        for n in range(-W1_AHEAD, N_CHUNKS + 1):
+            if exists(n - 1):
+                finish(n - 1)
+            if exists(n + W1_AHEAD):
+                transpose_w1(n + W1_AHEAD)
+            if exists(n):
+                regroup_h(n)
+                quantise_wb(n)
+                quantise_h(n)
+            if exists(n + W1_AHEAD):
+                quantise_w1(n + W1_AHEAD)
+            if exists(n + STAGE1_AHEAD):
+                stage1(n + STAGE1_AHEAD)
+            if exists(n + WB_AHEAD):
+                transpose_wb(n + WB_AHEAD)
+            if exists(n):
+                stage2(n)
+            if n in (1, 2):
+                spread_bb(2 * n + 2, False)

@@ -10,8 +10,6 @@ U8 = mybir.dt.uint8
 FP8X4 = mybir.dt.float8_e4m3fn_x4
 RELU = mybir.ActivationFunctionType.Relu
 ADD = mybir.AluOpType.add
-MAX = mybir.AluOpType.max
-MULT = mybir.AluOpType.mult
 
 P = 128
 BATCH = 512
@@ -26,7 +24,7 @@ W1_AHEAD = 2
 WB_AHEAD = 1
 STAGE1_AHEAD = 1
 HELPED = 1
-SCALAR_RELU = (5, 6, 7)
+SCALAR_QUARTERS = (1, 1, 1, 1, 1, 2, 4, 4)
 
 FLOPS = 2 * BATCH * K1 * HID + 2 * BATCH * CHUNK * HID
 
@@ -157,7 +155,7 @@ def tile_blockdiagmnistconvertible_pa_kernel(tc, x, W1, b1, Wb, bb, out):
             pairs = grouped[:].bitcast(F32)
             for t in range(TILES):
                 bank = transpose_words(words, BANK * t)
-                copy_out(t == 3 or n < HELPED and t == 1,
+                copy_out(n < HELPED and t % 2 == 1,
                          pairs[:, BANK * t:BANK * (t + 1)].rearrange("p (g c u) -> p g c u", g=2, u=2),
                          bank[:].rearrange("p (g u c) -> p g c u", g=2, u=2))
 
@@ -220,25 +218,34 @@ def tile_blockdiagmnistconvertible_pa_kernel(tc, x, W1, b1, Wb, bb, out):
                                     lhsT_scale=h_scales[n][:, b * P:(b + 1) * P],
                                     rhs=wb_codes[n][:].bitcast(FP8X4), rhs_scale=wb_scales[n][:], start=True, stop=True)
 
-        def finish(n):
+        def store(n, first, last):
+            nc.sync.dma_start(out=out_rows[:, first:last, n * CHUNK:(n + 1) * CHUNK],
+                              in_=out_sb[n][:].rearrange("c (b o) -> c b o", b=TILES)[:, first:last, :])
+
+        def add_bb(n):
             result = slow.tile([P, TILES * CHUNK], F32, tag="out_sb")
             out_sb[n] = result
             for b in range(TILES):
                 part = result[:, b * CHUNK:(b + 1) * CHUNK]
                 nc.vector.tensor_tensor(out=part, in0=products[(n, b)][:],
                                         in1=bb_all[:, n * CHUNK:(n + 1) * CHUNK], op=ADD)
-                if n in SCALAR_RELU:
+                if b < SCALAR_QUARTERS[n]:
                     nc.scalar.activation(out=part, in_=part, func=RELU)
-                else:
-                    nc.gpsimd.tensor_scalar(out=part, in0=part, scalar1=0.0, scalar2=1.0, op0=MAX, op1=MULT)
-                nc.sync.dma_start(out=out_rows[:, b, n * CHUNK:(n + 1) * CHUNK], in_=part)
+                    store(n, b, b + 1)
+
+        def relu_rest(n):
+            first = SCALAR_QUARTERS[n]
+            if first < TILES:
+                part = out_sb[n][:, first * CHUNK:]
+                nc.vector.tensor_scalar_max(out=part, in0=part, scalar1=0.0)
+                store(n, first, TILES)
 
         def exists(n):
             return 0 <= n < N_CHUNKS
 
         for n in range(-W1_AHEAD, N_CHUNKS + 1):
             if exists(n - 1):
-                finish(n - 1)
+                add_bb(n - 1)
             if exists(n + W1_AHEAD):
                 transpose_w1(n + W1_AHEAD)
             if exists(n):
@@ -247,6 +254,8 @@ def tile_blockdiagmnistconvertible_pa_kernel(tc, x, W1, b1, Wb, bb, out):
                 quantise_h(n)
             if exists(n + W1_AHEAD):
                 quantise_w1(n + W1_AHEAD)
+            if exists(n - 1):
+                relu_rest(n - 1)
             if exists(n + STAGE1_AHEAD):
                 stage1(n + STAGE1_AHEAD)
             if exists(n + WB_AHEAD):

@@ -42,13 +42,6 @@ def tile_blockdiagmnistconvertible_pa_kernel(tc, x, W1, b1, Wb, bb, out):
 
         ident = const.tile([P, P], F32)
         make_identity(nc, ident[:])
-        b1_rows = const.tile([P, CHUNK], BF16)
-        nc.vector.memset(b1_rows[:], 0.0)
-        bb_rows = const.tile([P, CHUNK], BF16)
-        nc.vector.memset(bb_rows[:], 0.0)
-        nc.sync.dma_start(out=b1_rows[0:N_CHUNKS, :], in_=b1.rearrange("(n w) -> n w", w=CHUNK))
-        nc.sync.dma_start(out=bb_rows[0:N_CHUNKS, :], in_=bb.rearrange("(n o) -> n o", o=CHUNK))
-
         x_sb = const.tile([P, TILES * K1], BF16)
         x_src = x.rearrange("(c b) k -> c b k", b=TILES)
         x_dst = x_sb[:].rearrange("c (b k) -> c b k", b=TILES)
@@ -75,14 +68,22 @@ def tile_blockdiagmnistconvertible_pa_kernel(tc, x, W1, b1, Wb, bb, out):
             nc.sync.dma_start(out=wb_tile[:].rearrange("c (j k) -> c j k", j=TILES),
                               in_=Wb[n].rearrange("(c j) k -> c j k", j=TILES))
 
+        b1_col = const.tile([P, TILES * N_CHUNKS], BF16)
+        bb_all = const.tile([P, HID], BF16)
+
+        def load_bb(n0, n1):
+            nc.sync.dma_start(out=bb_all[:, n0 * CHUNK:n1 * CHUNK], in_=bb[n0 * CHUNK:n1 * CHUNK].partition_broadcast(P))
+
         load_w1(0)
+        nc.sync.dma_start(out=b1_col[:].rearrange("p (n t) -> p n t", t=TILES),
+                          in_=b1.rearrange("(n p t) -> p n t", p=P, t=TILES))
         for n in range(1, N_CHUNKS):
             load_w1(n)
             load_wb(n - 1)
+            if n == 2:
+                load_bb(0, 4)
         load_wb(N_CHUNKS - 1)
-
-        ident_bf = const.tile([P, P], BF16)
-        nc.vector.tensor_copy(out=ident_bf[:], in_=ident[:])
+        load_bb(4, N_CHUNKS)
 
         def copy_out(on_vector, dst, src):
             if on_vector:
@@ -97,29 +98,6 @@ def tile_blockdiagmnistconvertible_pa_kernel(tc, x, W1, b1, Wb, bb, out):
                 nc.tensor.transpose(out=bank[:, P * i:P * (i + 1)], in_=words[:, lo + i % 2:lo + 2 * P:2],
                                     identity=ident[:])
             return bank
-
-        b1_bank = psum.tile([P, BANK], F32, tag="bank")
-        for u in range(2):
-            nc.tensor.transpose(out=b1_bank[:, u * P:(u + 1) * P], in_=b1_rows[:].bitcast(F32)[:, u:2 * P:2],
-                                identity=ident[:])
-        b1_words = const.tile([P, 2 * N_CHUNKS], F32)
-        nc.vector.tensor_copy(out=b1_words[:].rearrange("p (n u) -> p n u", u=2),
-                              in_=b1_bank[:, 0:2 * P].rearrange("p (u r) -> p r u", u=2)[:, 0:N_CHUNKS, :])
-        b1_col = const.tile([P, TILES * N_CHUNKS], F32)
-        nc.vector.tensor_copy(out=b1_col[:], in_=b1_words[:].bitcast(BF16))
-
-        bb_all = const.tile([P, HID], BF16)
-
-        def spread_bb(n0, on_vector):
-            wide = psum.tile([P, 2 * CHUNK], BF16, tag="bank")
-            for s in range(2):
-                nc.tensor.matmul(out=wide[:, s * CHUNK:(s + 1) * CHUNK],
-                                 lhsT=ident_bf[:, n0 + s:n0 + s + 1].to_broadcast([P, P]),
-                                 rhs=bb_rows[:], start=True, stop=True)
-            copy_out(on_vector, bb_all[:, n0 * CHUNK:(n0 + 2) * CHUNK], wide[:])
-
-        spread_bb(0, True)
-        spread_bb(2, False)
 
         x_grouped = const.tile([P, TILES * K1], BF16, align_bytes=64)
         x_codes = const.tile([P, K1], U32, align_bytes=64)
@@ -262,5 +240,3 @@ def tile_blockdiagmnistconvertible_pa_kernel(tc, x, W1, b1, Wb, bb, out):
                 transpose_wb(n + WB_AHEAD)
             if exists(n):
                 stage2(n)
-            if n in (1, 2):
-                spread_bb(2 * n + 2, False)

@@ -20,11 +20,11 @@ N_CHUNKS = HID // CHUNK
 TILES = 4
 BANK = 512
 PSUM_BANKS = 8
-W1_AHEAD = 2
-WB_AHEAD = 1
-STAGE1_AHEAD = 1
+W1_AHEAD = 3
+WB_AHEAD = 2
+STAGE1_AHEAD = 2
 HELPED = 1
-SCALAR_QUARTERS = (1, 1, 1, 1, 1, 2, 4, 4)
+SCALAR_QUARTERS = (1, 1, 1, 1, 1, 4, 4, 4)
 
 FLOPS = 2 * BATCH * K1 * HID + 2 * BATCH * CHUNK * HID
 
@@ -126,12 +126,13 @@ def tile_blockdiagmnistconvertible_pa_kernel(tc, x, W1, b1, Wb, bb, out):
         out_sb = {}
         out_rows = out.rearrange("(c b) o -> c b o", b=TILES)
 
-        def transpose_w1(n):
-            grouped = work.tile([P, TILES * K1], BF16, align_bytes=64, tag="w1_grouped")
-            w1_grouped[n] = grouped
+        def transpose_w1(n, half):
+            if half == 0:
+                grouped = work.tile([P, TILES * K1], BF16, align_bytes=64, tag="w1_grouped")
+                w1_grouped[n] = grouped
             words = w1_sb[n][:].bitcast(F32)
-            pairs = grouped[:].bitcast(F32)
-            for t in range(TILES):
+            pairs = w1_grouped[n][:].bitcast(F32)
+            for t in (2 * half, 2 * half + 1):
                 bank = transpose_words(words, BANK * t)
                 copy_out(n < HELPED and t % 2 == 1,
                          pairs[:, BANK * t:BANK * (t + 1)].rearrange("p (g c u) -> p g c u", g=2, u=2),
@@ -160,10 +161,11 @@ def tile_blockdiagmnistconvertible_pa_kernel(tc, x, W1, b1, Wb, bb, out):
             wb_scales[n] = scales
             nc.vector.quantize_mx(out=codes[:].bitcast(FP8X4), scales=scales[:], in_=wb_grouped[n][:])
 
-        def stage1(n):
-            planes = work.tile([P, TILES * BATCH], BF16, tag="h_planes")
-            h_planes[n] = planes
-            for t in range(TILES):
+        def stage1(n, half):
+            if half == 0:
+                planes = work.tile([P, TILES * BATCH], BF16, tag="h_planes")
+                h_planes[n] = planes
+            for t in (2 * half, 2 * half + 1):
                 acc = psum.tile([P, BATCH], F32, tag="bank")
                 for g in range(2):
                     lo = (2 * t + g) * P
@@ -172,7 +174,7 @@ def tile_blockdiagmnistconvertible_pa_kernel(tc, x, W1, b1, Wb, bb, out):
                                         rhs=x_codes[:, g * BATCH:(g + 1) * BATCH].bitcast(FP8X4),
                                         rhs_scale=x_scales[:, g * BATCH:(g + 1) * BATCH],
                                         start=(g == 0), stop=(g == 1))
-                nc.scalar.activation(out=planes[:, t * BATCH:(t + 1) * BATCH], in_=acc[:], func=RELU,
+                nc.scalar.activation(out=h_planes[n][:, t * BATCH:(t + 1) * BATCH], in_=acc[:], func=RELU,
                                      bias=b1_col[:, TILES * n + t:TILES * n + t + 1], scale=1.0)
 
         def regroup_h(n):
@@ -200,43 +202,43 @@ def tile_blockdiagmnistconvertible_pa_kernel(tc, x, W1, b1, Wb, bb, out):
             nc.sync.dma_start(out=out_rows[:, first:last, n * CHUNK:(n + 1) * CHUNK],
                               in_=out_sb[n][:].rearrange("c (b o) -> c b o", b=TILES)[:, first:last, :])
 
-        def add_bb(n):
-            result = slow.tile([P, TILES * CHUNK], F32, tag="out_sb")
-            out_sb[n] = result
-            for b in range(TILES):
-                part = result[:, b * CHUNK:(b + 1) * CHUNK]
-                nc.vector.tensor_tensor(out=part, in0=products[(n, b)][:],
+        def add_bb(n, half):
+            if half == 0:
+                result = slow.tile([P, TILES * CHUNK], F32, tag="out_sb")
+                out_sb[n] = result
+            for b in (2 * half, 2 * half + 1):
+                nc.vector.tensor_tensor(out=out_sb[n][:, b * CHUNK:(b + 1) * CHUNK], in0=products[(n, b)][:],
                                         in1=bb_all[:, n * CHUNK:(n + 1) * CHUNK], op=ADD)
-                if b < SCALAR_QUARTERS[n]:
-                    nc.scalar.activation(out=part, in_=part, func=RELU)
-                    store(n, b, b + 1)
 
-        def relu_rest(n):
+        def relu_on_scalar(n):
+            for b in range(SCALAR_QUARTERS[n]):
+                part = out_sb[n][:, b * CHUNK:(b + 1) * CHUNK]
+                nc.scalar.activation(out=part, in_=part, func=RELU)
+                store(n, b, b + 1)
+
+        def relu_on_vector(n):
             first = SCALAR_QUARTERS[n]
             if first < TILES:
                 part = out_sb[n][:, first * CHUNK:]
                 nc.vector.tensor_scalar_max(out=part, in0=part, scalar1=0.0)
                 store(n, first, TILES)
 
-        def exists(n):
-            return 0 <= n < N_CHUNKS
+        def step(stage, n, *half):
+            if 0 <= n < N_CHUNKS:
+                stage(n, *half)
 
         for n in range(-W1_AHEAD, N_CHUNKS + 1):
-            if exists(n - 1):
-                add_bb(n - 1)
-            if exists(n + W1_AHEAD):
-                transpose_w1(n + W1_AHEAD)
-            if exists(n):
-                regroup_h(n)
-                quantise_wb(n)
-                quantise_h(n)
-            if exists(n + W1_AHEAD):
-                quantise_w1(n + W1_AHEAD)
-            if exists(n - 1):
-                relu_rest(n - 1)
-            if exists(n + STAGE1_AHEAD):
-                stage1(n + STAGE1_AHEAD)
-            if exists(n + WB_AHEAD):
-                transpose_wb(n + WB_AHEAD)
-            if exists(n):
-                stage2(n)
+            step(quantise_wb, n + 1)
+            step(regroup_h, n + 1)
+            step(transpose_w1, n + W1_AHEAD, 0)
+            step(relu_on_scalar, n - 1)
+            step(stage2, n)
+            step(add_bb, n, 0)
+            step(transpose_w1, n + W1_AHEAD, 1)
+            step(quantise_h, n + 1)
+            step(add_bb, n, 1)
+            step(stage1, n + STAGE1_AHEAD, 0)
+            step(transpose_wb, n + WB_AHEAD)
+            step(quantise_w1, n + W1_AHEAD)
+            step(stage1, n + STAGE1_AHEAD, 1)
+            step(relu_on_vector, n)

@@ -23,6 +23,7 @@ PSUM_BANKS = 8
 W1_AHEAD = 3
 WB_AHEAD = 2
 STAGE1_AHEAD = 2
+SPLIT_LOADS = 3
 HELPED = 1
 SCALAR_QUARTERS = (1, 1, 1, 1, 1, 4, 4, 4)
 
@@ -45,8 +46,8 @@ def tile_blockdiagmnistconvertible_pa_kernel(tc, x, W1, b1, Wb, bb, out):
         x_sb = const.tile([P, TILES * K1], BF16)
         x_src = x.rearrange("(c b) k -> c b k", b=TILES)
         x_dst = x_sb[:].rearrange("c (b k) -> c b k", b=TILES)
-        for half in range(2):
-            nc.sync.dma_start(out=x_dst[:, 2 * half:2 * half + 2, :], in_=x_src[:, 2 * half:2 * half + 2, :])
+        for b in range(TILES):
+            nc.sync.dma_start(out=x_dst[:, b, :], in_=x_src[:, b, :])
 
         w1_sb = {}
         wb_sb = {}
@@ -56,7 +57,7 @@ def tile_blockdiagmnistconvertible_pa_kernel(tc, x, W1, b1, Wb, bb, out):
             w1_sb[n] = w1_tile
             src = W1[n * CHUNK:(n + 1) * CHUNK, :].rearrange("(p t) k -> p t k", t=TILES)
             dst = w1_tile[:].rearrange("p (t k) -> p t k", t=TILES)
-            if n == 0:
+            if n < SPLIT_LOADS:
                 for half in range(2):
                     nc.sync.dma_start(out=dst[:, 2 * half:2 * half + 2, :], in_=src[:, 2 * half:2 * half + 2, :])
             else:
@@ -75,10 +76,11 @@ def tile_blockdiagmnistconvertible_pa_kernel(tc, x, W1, b1, Wb, bb, out):
             nc.sync.dma_start(out=bb_all[:, n0 * CHUNK:n1 * CHUNK], in_=bb[n0 * CHUNK:n1 * CHUNK].partition_broadcast(P))
 
         load_w1(0)
-        nc.sync.dma_start(out=b1_col[:].rearrange("p (n t) -> p n t", t=TILES),
-                          in_=b1.rearrange("(n p t) -> p n t", p=P, t=TILES))
         for n in range(1, N_CHUNKS):
             load_w1(n)
+            if n == 1:
+                nc.sync.dma_start(out=b1_col[:].rearrange("p (n t) -> p n t", t=TILES),
+                                  in_=b1.rearrange("(n p t) -> p n t", p=P, t=TILES))
             load_wb(n - 1)
             if n == 2:
                 load_bb(0, 4)
@@ -137,13 +139,19 @@ def tile_blockdiagmnistconvertible_pa_kernel(tc, x, W1, b1, Wb, bb, out):
                 copy_out(n < HELPED and t % 2 == 1,
                          pairs[:, BANK * t:BANK * (t + 1)].rearrange("p (g c u) -> p g c u", g=2, u=2),
                          bank[:].rearrange("p (g u c) -> p g c u", g=2, u=2))
+            if n == 0:
+                quantise_w1(n, 2 * half, 2 * half + 2)
 
-        def quantise_w1(n):
-            codes = work.tile([P, K1], U32, align_bytes=64, tag="w1_codes")
-            scales = work.tile([P, K1], U8, align_bytes=64, tag="w1_scales")
-            w1_codes[n] = codes
-            w1_scales[n] = scales
-            nc.vector.quantize_mx(out=codes[:].bitcast(FP8X4), scales=scales[:], in_=w1_grouped[n][:])
+        def quantise_w1(n, first=0, last=TILES):
+            if first == 0:
+                codes = work.tile([P, K1], U32, align_bytes=64, tag="w1_codes")
+                scales = work.tile([P, K1], U8, align_bytes=64, tag="w1_scales")
+                w1_codes[n] = codes
+                w1_scales[n] = scales
+            width = K1 // TILES
+            cols = slice(first * width, last * width)
+            nc.vector.quantize_mx(out=w1_codes[n][:, cols].bitcast(FP8X4), scales=w1_scales[n][:, cols],
+                                  in_=w1_grouped[n][:, first * K1:last * K1])
 
         def transpose_wb(n):
             grouped = work.tile([P, TILES * CHUNK], BF16, align_bytes=64, tag="wb_grouped")
@@ -239,6 +247,7 @@ def tile_blockdiagmnistconvertible_pa_kernel(tc, x, W1, b1, Wb, bb, out):
             step(add_bb, n, 1)
             step(stage1, n + STAGE1_AHEAD, 0)
             step(transpose_wb, n + WB_AHEAD)
-            step(quantise_w1, n + W1_AHEAD)
+            if n + W1_AHEAD > 0:
+                step(quantise_w1, n + W1_AHEAD)
             step(stage1, n + STAGE1_AHEAD, 1)
             step(relu_on_vector, n)

@@ -43,6 +43,13 @@ def tile_blockdiagmnistconvertible_pa_kernel(tc, x, W1, b1, Wb, bb, out):
 
         ident = const.tile([P, P], F32)
         make_identity(nc, ident[:])
+        bias_rows = const.tile([P, 2 * CHUNK], BF16)
+        nc.vector.memset(bias_rows[:].bitcast(F32), 0.0)
+        b1_rows = bias_rows[:, 0:CHUNK]
+        bb_rows = bias_rows[:, CHUNK:2 * CHUNK]
+        nc.scalar.dma_start(out=b1_rows[0:N_CHUNKS, :], in_=b1.rearrange("(n w) -> n w", w=CHUNK))
+        nc.scalar.dma_start(out=bb_rows[0:N_CHUNKS, :], in_=bb.rearrange("(n o) -> n o", o=CHUNK))
+
         x_sb = const.tile([P, TILES * K1], BF16)
         x_src = x.rearrange("(c b) k -> c b k", b=TILES)
         x_dst = x_sb[:].rearrange("c (b k) -> c b k", b=TILES)
@@ -69,23 +76,11 @@ def tile_blockdiagmnistconvertible_pa_kernel(tc, x, W1, b1, Wb, bb, out):
             nc.sync.dma_start(out=wb_tile[:].rearrange("c (j k) -> c j k", j=TILES),
                               in_=Wb[n].rearrange("(c j) k -> c j k", j=TILES))
 
-        b1_col = const.tile([P, TILES * N_CHUNKS], BF16)
-        bb_all = const.tile([P, HID], BF16)
-
-        def load_bb(n0, n1):
-            nc.sync.dma_start(out=bb_all[:, n0 * CHUNK:n1 * CHUNK], in_=bb[n0 * CHUNK:n1 * CHUNK].partition_broadcast(P))
-
         load_w1(0)
         for n in range(1, N_CHUNKS):
             load_w1(n)
-            if n == 1:
-                nc.sync.dma_start(out=b1_col[:].rearrange("p (n t) -> p n t", t=TILES),
-                                  in_=b1.rearrange("(n p t) -> p n t", p=P, t=TILES))
             load_wb(n - 1)
-            if n == 2:
-                load_bb(0, 4)
         load_wb(N_CHUNKS - 1)
-        load_bb(4, N_CHUNKS)
 
         def copy_out(on_vector, dst, src):
             if on_vector:
@@ -101,6 +96,29 @@ def tile_blockdiagmnistconvertible_pa_kernel(tc, x, W1, b1, Wb, bb, out):
                                     identity=ident[:])
             return bank
 
+        ident_bf = const.tile([P, P], BF16)
+        nc.vector.tensor_copy(out=ident_bf[:], in_=ident[:])
+
+        b1_col = const.tile([P, TILES * N_CHUNKS], BF16)
+
+        def spread_b1():
+            b1_bank = psum.tile([P, BANK], F32, tag="bank")
+            for u in range(2):
+                nc.tensor.transpose(out=b1_bank[:, u * P:(u + 1) * P], in_=b1_rows.bitcast(F32)[:, u:2 * P:2],
+                                    identity=ident[:])
+            nc.vector.tensor_copy(out=b1_col[:].bitcast(F32).rearrange("p (n u) -> p n u", u=2),
+                                  in_=b1_bank[:, 0:2 * P].rearrange("p (u r) -> p r u", u=2)[:, 0:N_CHUNKS, :])
+
+        bb_all = const.tile([P, HID], BF16)
+
+        def spread_bb(n0, on_vector):
+            wide = psum.tile([P, 2 * CHUNK], BF16, tag="bank")
+            for s in range(2):
+                nc.tensor.matmul(out=wide[:, s * CHUNK:(s + 1) * CHUNK],
+                                 lhsT=ident_bf[:, n0 + s:n0 + s + 1].to_broadcast([P, P]),
+                                 rhs=bb_rows, start=True, stop=True)
+            copy_out(on_vector, bb_all[:, n0 * CHUNK:(n0 + 2) * CHUNK], wide[:])
+
         x_grouped = const.tile([P, TILES * K1], BF16, align_bytes=64)
         x_codes = const.tile([P, K1], U32, align_bytes=64)
         x_scales = const.tile([P, K1], U8, align_bytes=64)
@@ -109,6 +127,9 @@ def tile_blockdiagmnistconvertible_pa_kernel(tc, x, W1, b1, Wb, bb, out):
         for b in range(TILES):
             bank = transpose_words(x_words, BANK * b)
             copy_out(b % 2 == 1, x_pairs[:, :, b, :, :], bank[:].rearrange("p (g u c) -> p g c u", g=2, u=2))
+            if b % 2 == 1:
+                spread_bb(b - 1, b == 1)
+        spread_b1()
         for g in range(2):
             nc.vector.quantize_mx(out=x_codes[:, g * BATCH:(g + 1) * BATCH].bitcast(FP8X4),
                                   scales=x_scales[:, g * BATCH:(g + 1) * BATCH],
@@ -139,6 +160,8 @@ def tile_blockdiagmnistconvertible_pa_kernel(tc, x, W1, b1, Wb, bb, out):
                 copy_out(n < HELPED and t % 2 == 1,
                          pairs[:, BANK * t:BANK * (t + 1)].rearrange("p (g c u) -> p g c u", g=2, u=2),
                          bank[:].rearrange("p (g u c) -> p g c u", g=2, u=2))
+            if n == 0:
+                spread_bb(4 + 2 * half, half == 0)
             if n == 0:
                 quantise_w1(n, 2 * half, 2 * half + 2)
 

@@ -10,6 +10,8 @@ U8 = mybir.dt.uint8
 FP8X4 = mybir.dt.float8_e4m3fn_x4
 RELU = mybir.ActivationFunctionType.Relu
 ADD = mybir.AluOpType.add
+MAX = mybir.AluOpType.max
+MIN = mybir.AluOpType.min
 
 P = 128
 BATCH = 512
@@ -24,8 +26,11 @@ W1_AHEAD = 3
 WB_AHEAD = 2
 STAGE1_AHEAD = 2
 SPLIT_LOADS = 3
+SPLIT_W1 = (2,)
+SPLIT_WB = (1, 2)
 HELPED = 1
-SCALAR_QUARTERS = (1, 1, 1, 1, 1, 4, 4, 4)
+RELU_BY = ("GGSV",) * 5 + ("GGSS", "GGSS", "SSSS")
+FLOAT32_MAX = 3.4028234663852886e38
 
 FLOPS = 2 * BATCH * K1 * HID + 2 * BATCH * CHUNK * HID
 
@@ -38,6 +43,7 @@ def tile_blockdiagmnistconvertible_pa_kernel(tc, x, W1, b1, Wb, bb, out):
         wb_pool = ctx.enter_context(tc.tile_pool(name="wb_pool", bufs=N_CHUNKS))
         work = ctx.enter_context(tc.tile_pool(name="work", bufs=2))
         slow = ctx.enter_context(tc.tile_pool(name="slow", bufs=3))
+        out_pool = ctx.enter_context(tc.tile_pool(name="out_pool", bufs=4))
         psum = ctx.enter_context(tc.psum_pool(name="psum", bufs=PSUM_BANKS))
         ctx.enter_context(tc.manual_schedule())
 
@@ -47,14 +53,15 @@ def tile_blockdiagmnistconvertible_pa_kernel(tc, x, W1, b1, Wb, bb, out):
         nc.vector.memset(bias_rows[:].bitcast(F32), 0.0)
         b1_rows = bias_rows[:, 0:CHUNK]
         bb_rows = bias_rows[:, CHUNK:2 * CHUNK]
-        nc.scalar.dma_start(out=b1_rows[0:N_CHUNKS, :], in_=b1.rearrange("(n w) -> n w", w=CHUNK))
-        nc.scalar.dma_start(out=bb_rows[0:N_CHUNKS, :], in_=bb.rearrange("(n o) -> n o", o=CHUNK))
 
         x_sb = const.tile([P, TILES * K1], BF16)
         x_src = x.rearrange("(c b) k -> c b k", b=TILES)
         x_dst = x_sb[:].rearrange("c (b k) -> c b k", b=TILES)
         for b in range(TILES):
             nc.sync.dma_start(out=x_dst[:, b, :], in_=x_src[:, b, :])
+            if b == 1:
+                nc.sync.dma_start(out=b1_rows[0:N_CHUNKS, :], in_=b1.rearrange("(n w) -> n w", w=CHUNK))
+                nc.sync.dma_start(out=bb_rows[0:N_CHUNKS, :], in_=bb.rearrange("(n o) -> n o", o=CHUNK))
 
         w1_sb = {}
         wb_sb = {}
@@ -88,12 +95,18 @@ def tile_blockdiagmnistconvertible_pa_kernel(tc, x, W1, b1, Wb, bb, out):
             else:
                 nc.scalar.copy(out=dst, in_=src)
 
-        def transpose_words(words, first):
+        def split_words(raw, tag):
+            split = const.tile([P, raw.shape[1]], BF16, tag=tag)
+            nc.vector.tensor_copy(out=split[:].bitcast(F32).rearrange("r (s u p) -> r s u p", u=2, p=P),
+                                  in_=raw[:].bitcast(F32).rearrange("r (s p u) -> r s u p", u=2, p=P))
+            return split
+
+        def transpose_words(words, first, split=False):
             bank = psum.tile([P, BANK], F32, tag="bank")
             for i in range(4):
                 lo = first + 2 * P * (i // 2)
-                nc.tensor.transpose(out=bank[:, P * i:P * (i + 1)], in_=words[:, lo + i % 2:lo + 2 * P:2],
-                                    identity=ident[:])
+                cols = slice(lo + P * (i % 2), lo + P * (i % 2) + P) if split else slice(lo + i % 2, lo + 2 * P, 2)
+                nc.tensor.transpose(out=bank[:, P * i:P * (i + 1)], in_=words[:, cols], identity=ident[:])
             return bank
 
         ident_bf = const.tile([P, P], BF16)
@@ -149,6 +162,14 @@ def tile_blockdiagmnistconvertible_pa_kernel(tc, x, W1, b1, Wb, bb, out):
         out_sb = {}
         out_rows = out.rearrange("(c b) o -> c b o", b=TILES)
 
+        def split_w1(n):
+            if n in SPLIT_W1:
+                w1_sb[n] = split_words(w1_sb[n], "w1_split_%d" % n)
+
+        def split_wb(n):
+            if n in SPLIT_WB:
+                wb_sb[n] = split_words(wb_sb[n], "wb_split_%d" % n)
+
         def transpose_w1(n, half):
             if half == 0:
                 grouped = work.tile([P, TILES * K1], BF16, align_bytes=64, tag="w1_grouped")
@@ -156,7 +177,7 @@ def tile_blockdiagmnistconvertible_pa_kernel(tc, x, W1, b1, Wb, bb, out):
             words = w1_sb[n][:].bitcast(F32)
             pairs = w1_grouped[n][:].bitcast(F32)
             for t in (2 * half, 2 * half + 1):
-                bank = transpose_words(words, BANK * t)
+                bank = transpose_words(words, BANK * t, n in SPLIT_W1)
                 copy_out(n < HELPED and t % 2 == 1,
                          pairs[:, BANK * t:BANK * (t + 1)].rearrange("p (g c u) -> p g c u", g=2, u=2),
                          bank[:].rearrange("p (g u c) -> p g c u", g=2, u=2))
@@ -182,7 +203,7 @@ def tile_blockdiagmnistconvertible_pa_kernel(tc, x, W1, b1, Wb, bb, out):
             words = wb_sb[n][:].bitcast(F32)
             pairs = grouped[:].bitcast(F32).rearrange("p (c hi lu) -> p c hi lu", hi=2, lu=4)
             for hi in range(2):
-                bank = transpose_words(words, BANK * hi)
+                bank = transpose_words(words, BANK * hi, n in SPLIT_WB)
                 copy_out(n < HELPED, pairs[:, :, hi, :], bank[:].rearrange("p (lu c) -> p c lu", lu=4))
 
         def quantise_wb(n):
@@ -211,8 +232,13 @@ def tile_blockdiagmnistconvertible_pa_kernel(tc, x, W1, b1, Wb, bb, out):
         def regroup_h(n):
             grouped = work.tile([P, TILES * BATCH], BF16, align_bytes=64, tag="h_grouped")
             h_grouped[n] = grouped
-            nc.vector.tensor_copy(out=grouped[:].rearrange("p (run i t) -> p run t i", i=4, t=TILES),
-                                  in_=h_planes[n][:].rearrange("p (t run i) -> p run t i", t=TILES, i=4))
+            dst = grouped[:].rearrange("p (run i t) -> p run t i", i=4, t=TILES)
+            src = h_planes[n][:].rearrange("p (t run i) -> p run t i", t=TILES, i=4)
+            runs = BATCH // 4
+            mine = runs if n < N_CHUNKS - 1 else 5 * runs // 8
+            nc.vector.tensor_copy(out=dst[:, :mine], in_=src[:, :mine])
+            if mine < runs:
+                nc.scalar.copy(out=dst[:, mine:], in_=src[:, mine:])
 
         def quantise_h(n):
             codes = work.tile([P, BATCH], U32, align_bytes=64, tag="h_codes")
@@ -229,48 +255,66 @@ def tile_blockdiagmnistconvertible_pa_kernel(tc, x, W1, b1, Wb, bb, out):
                                     lhsT_scale=h_scales[n][:, b * P:(b + 1) * P],
                                     rhs=wb_codes[n][:].bitcast(FP8X4), rhs_scale=wb_scales[n][:], start=True, stop=True)
 
-        def store(n, first, last):
-            nc.sync.dma_start(out=out_rows[:, first:last, n * CHUNK:(n + 1) * CHUNK],
-                              in_=out_sb[n][:].rearrange("c (b o) -> c b o", b=TILES)[:, first:last, :])
+        def pieces(n):
+            whole = [(b, 0, CHUNK, RELU_BY[n][b]) for b in range(TILES)]
+            if n < N_CHUNKS - 1:
+                return whole
+            b, lo, hi, engine = whole[-1]
+            return whole[:-1] + [(b, lo, hi // 2, engine), (b, hi // 2, hi, engine)]
 
-        def add_bb(n, half):
-            if half == 0:
-                result = slow.tile([P, TILES * CHUNK], F32, tag="out_sb")
-                out_sb[n] = result
-            for b in (2 * half, 2 * half + 1):
-                nc.vector.tensor_tensor(out=out_sb[n][:, b * CHUNK:(b + 1) * CHUNK], in0=products[(n, b)][:],
-                                        in1=bb_all[:, n * CHUNK:(n + 1) * CHUNK], op=ADD)
+        def store(n, b, lo, hi):
+            nc.sync.dma_start(out=out_rows[:, b, n * CHUNK + lo:n * CHUNK + hi],
+                              in_=out_sb[n][:, b * CHUNK + lo:b * CHUNK + hi])
+
+        def add_bb(n):
+            result = out_pool.tile([P, TILES * CHUNK], F32, tag="out_sb")
+            out_sb[n] = result
+            for b, lo, hi, engine in pieces(n):
+                part = result[:, b * CHUNK + lo:b * CHUNK + hi]
+                nc.vector.tensor_tensor(out=part, in0=products[(n, b)][:, lo:hi],
+                                        in1=bb_all[:, n * CHUNK + lo:n * CHUNK + hi], op=ADD)
+                if engine == "G":
+                    nc.gpsimd.tensor_scalar(out=part, in0=part, scalar1=FLOAT32_MAX, scalar2=0.0, op0=MIN, op1=MAX)
+                    store(n, b, lo, hi)
 
         def relu_on_scalar(n):
-            for b in range(SCALAR_QUARTERS[n]):
-                part = out_sb[n][:, b * CHUNK:(b + 1) * CHUNK]
-                nc.scalar.activation(out=part, in_=part, func=RELU)
-                store(n, b, b + 1)
+            for b, lo, hi, engine in pieces(n):
+                if engine == "S":
+                    part = out_sb[n][:, b * CHUNK + lo:b * CHUNK + hi]
+                    nc.scalar.activation(out=part, in_=part, func=RELU)
+                    store(n, b, lo, hi)
 
         def relu_on_vector(n):
-            first = SCALAR_QUARTERS[n]
-            if first < TILES:
-                part = out_sb[n][:, first * CHUNK:]
-                nc.vector.tensor_scalar_max(out=part, in0=part, scalar1=0.0)
-                store(n, first, TILES)
+            for b, lo, hi, engine in pieces(n):
+                if engine == "V":
+                    part = out_sb[n][:, b * CHUNK + lo:b * CHUNK + hi]
+                    nc.vector.tensor_scalar_max(out=part, in0=part, scalar1=0.0)
+                    store(n, b, lo, hi)
 
         def step(stage, n, *half):
             if 0 <= n < N_CHUNKS:
                 stage(n, *half)
 
         for n in range(-W1_AHEAD, N_CHUNKS + 1):
+            tail = n + W1_AHEAD >= N_CHUNKS
             step(quantise_wb, n + 1)
             step(regroup_h, n + 1)
+            step(split_w1, n + W1_AHEAD + 1)
             step(transpose_w1, n + W1_AHEAD, 0)
             step(relu_on_scalar, n - 1)
             step(stage2, n)
-            step(add_bb, n, 0)
+            if tail:
+                step(relu_on_vector, n - 1)
+                step(quantise_h, n + 1)
+            step(add_bb, n)
             step(transpose_w1, n + W1_AHEAD, 1)
-            step(quantise_h, n + 1)
-            step(add_bb, n, 1)
+            if not tail:
+                step(quantise_h, n + 1)
             step(stage1, n + STAGE1_AHEAD, 0)
             step(transpose_wb, n + WB_AHEAD)
             if n + W1_AHEAD > 0:
                 step(quantise_w1, n + W1_AHEAD)
             step(stage1, n + STAGE1_AHEAD, 1)
-            step(relu_on_vector, n)
+            step(split_wb, n + WB_AHEAD + 1)
+            if n + W1_AHEAD + 1 < N_CHUNKS:
+                step(relu_on_vector, n)

from contextlib import ExitStack

import concourse.mybir as mybir
from concourse.masks import make_identity

F32 = mybir.dt.float32
BF16 = mybir.dt.bfloat16
U32 = mybir.dt.uint32
U8 = mybir.dt.uint8
FP8X4 = mybir.dt.float8_e4m3fn_x4
RELU = mybir.ActivationFunctionType.Relu
ADD = mybir.AluOpType.add
MAX = mybir.AluOpType.max
MIN = mybir.AluOpType.min

P = 128
BATCH = 512
K1 = 1024
HID = 4096
CHUNK = 512
N_CHUNKS = HID // CHUNK
TILES = 4
BANK = 512
PSUM_BANKS = 8
W1_AHEAD = 3
WB_AHEAD = 2
STAGE1_AHEAD = 2
SPLIT_LOADS = 3
SPLIT_W1 = (2,)
SPLIT_WB = (1, 2)
HELPED = 1
RELU_BY = ("GGSV",) * 5 + ("GGSS", "GGSS", "SSSS")
FLOAT32_MAX = 3.4028234663852886e38

FLOPS = 2 * BATCH * K1 * HID + 2 * BATCH * CHUNK * HID


def tile_blockdiagmnistconvertible_pa_kernel(tc, x, W1, b1, Wb, bb, out):
    nc = tc.nc
    with ExitStack() as ctx:
        const = ctx.enter_context(tc.tile_pool(name="const", bufs=1))
        w1_pool = ctx.enter_context(tc.tile_pool(name="w1_pool", bufs=N_CHUNKS))
        wb_pool = ctx.enter_context(tc.tile_pool(name="wb_pool", bufs=N_CHUNKS))
        work = ctx.enter_context(tc.tile_pool(name="work", bufs=2))
        slow = ctx.enter_context(tc.tile_pool(name="slow", bufs=3))
        out_pool = ctx.enter_context(tc.tile_pool(name="out_pool", bufs=4))
        psum = ctx.enter_context(tc.psum_pool(name="psum", bufs=PSUM_BANKS))
        ctx.enter_context(tc.manual_schedule())

        ident = const.tile([P, P], F32)
        make_identity(nc, ident[:])
        bias_rows = const.tile([P, 2 * CHUNK], BF16)
        nc.vector.memset(bias_rows[:].bitcast(F32), 0.0)
        b1_rows = bias_rows[:, 0:CHUNK]
        bb_rows = bias_rows[:, CHUNK:2 * CHUNK]

        x_sb = const.tile([P, TILES * K1], BF16)
        x_src = x.rearrange("(c b) k -> c b k", b=TILES)
        x_dst = x_sb[:].rearrange("c (b k) -> c b k", b=TILES)
        for b in range(TILES):
            nc.sync.dma_start(out=x_dst[:, b, :], in_=x_src[:, b, :])
            if b == 1:
                nc.sync.dma_start(out=b1_rows[0:N_CHUNKS, :], in_=b1.rearrange("(n w) -> n w", w=CHUNK))
                nc.sync.dma_start(out=bb_rows[0:N_CHUNKS, :], in_=bb.rearrange("(n o) -> n o", o=CHUNK))

        w1_sb = {}
        wb_sb = {}

        def load_w1(n):
            w1_tile = w1_pool.tile([P, TILES * K1], BF16)
            w1_sb[n] = w1_tile
            src = W1[n * CHUNK:(n + 1) * CHUNK, :].rearrange("(p t) k -> p t k", t=TILES)
            dst = w1_tile[:].rearrange("p (t k) -> p t k", t=TILES)
            if n < SPLIT_LOADS:
                for half in range(2):
                    nc.sync.dma_start(out=dst[:, 2 * half:2 * half + 2, :], in_=src[:, 2 * half:2 * half + 2, :])
            else:
                nc.sync.dma_start(out=dst, in_=src)

        def load_wb(n):
            wb_tile = wb_pool.tile([P, TILES * CHUNK], BF16)
            wb_sb[n] = wb_tile
            nc.sync.dma_start(out=wb_tile[:].rearrange("c (j k) -> c j k", j=TILES),
                              in_=Wb[n].rearrange("(c j) k -> c j k", j=TILES))

        load_w1(0)
        for n in range(1, N_CHUNKS):
            load_w1(n)
            load_wb(n - 1)
        load_wb(N_CHUNKS - 1)

        def copy_out(on_vector, dst, src):
            if on_vector:
                nc.vector.tensor_copy(out=dst, in_=src)
            else:
                nc.scalar.copy(out=dst, in_=src)

        def split_words(raw, tag):
            split = const.tile([P, raw.shape[1]], BF16, tag=tag)
            nc.vector.tensor_copy(out=split[:].bitcast(F32).rearrange("r (s u p) -> r s u p", u=2, p=P),
                                  in_=raw[:].bitcast(F32).rearrange("r (s p u) -> r s u p", u=2, p=P))
            return split

        def transpose_words(words, first, split=False):
            bank = psum.tile([P, BANK], F32, tag="bank")
            for i in range(4):
                lo = first + 2 * P * (i // 2)
                cols = slice(lo + P * (i % 2), lo + P * (i % 2) + P) if split else slice(lo + i % 2, lo + 2 * P, 2)
                nc.tensor.transpose(out=bank[:, P * i:P * (i + 1)], in_=words[:, cols], identity=ident[:])
            return bank

        ident_bf = const.tile([P, P], BF16)
        nc.vector.tensor_copy(out=ident_bf[:], in_=ident[:])

        b1_col = const.tile([P, TILES * N_CHUNKS], BF16)

        def spread_b1():
            b1_bank = psum.tile([P, BANK], F32, tag="bank")
            for u in range(2):
                nc.tensor.transpose(out=b1_bank[:, u * P:(u + 1) * P], in_=b1_rows.bitcast(F32)[:, u:2 * P:2],
                                    identity=ident[:])
            nc.vector.tensor_copy(out=b1_col[:].bitcast(F32).rearrange("p (n u) -> p n u", u=2),
                                  in_=b1_bank[:, 0:2 * P].rearrange("p (u r) -> p r u", u=2)[:, 0:N_CHUNKS, :])

        bb_all = const.tile([P, HID], BF16)

        def spread_bb(n0, on_vector):
            wide = psum.tile([P, 2 * CHUNK], BF16, tag="bank")
            for s in range(2):
                nc.tensor.matmul(out=wide[:, s * CHUNK:(s + 1) * CHUNK],
                                 lhsT=ident_bf[:, n0 + s:n0 + s + 1].to_broadcast([P, P]),
                                 rhs=bb_rows, start=True, stop=True)
            copy_out(on_vector, bb_all[:, n0 * CHUNK:(n0 + 2) * CHUNK], wide[:])

        x_grouped = const.tile([P, TILES * K1], BF16, align_bytes=64)
        x_codes = const.tile([P, K1], U32, align_bytes=64)
        x_scales = const.tile([P, K1], U8, align_bytes=64)
        x_words = x_sb[:].bitcast(F32)
        x_pairs = x_grouped[:].bitcast(F32).rearrange("p (g b c u) -> p g b c u", g=2, b=TILES, u=2)
        for b in range(TILES):
            bank = transpose_words(x_words, BANK * b)
            copy_out(b % 2 == 1, x_pairs[:, :, b, :, :], bank[:].rearrange("p (g u c) -> p g c u", g=2, u=2))
            if b % 2 == 1:
                spread_bb(b - 1, b == 1)
        spread_b1()
        for g in range(2):
            nc.vector.quantize_mx(out=x_codes[:, g * BATCH:(g + 1) * BATCH].bitcast(FP8X4),
                                  scales=x_scales[:, g * BATCH:(g + 1) * BATCH],
                                  in_=x_grouped[:, g * TILES * BATCH:(g + 1) * TILES * BATCH])

        w1_grouped = {}
        w1_codes = {}
        w1_scales = {}
        wb_grouped = {}
        wb_codes = {}
        wb_scales = {}
        h_planes = {}
        h_grouped = {}
        h_codes = {}
        h_scales = {}
        products = {}
        out_sb = {}
        out_rows = out.rearrange("(c b) o -> c b o", b=TILES)

        def split_w1(n):
            if n in SPLIT_W1:
                w1_sb[n] = split_words(w1_sb[n], "w1_split_%d" % n)

        def split_wb(n):
            if n in SPLIT_WB:
                wb_sb[n] = split_words(wb_sb[n], "wb_split_%d" % n)

        def transpose_w1(n, half):
            if half == 0:
                grouped = work.tile([P, TILES * K1], BF16, align_bytes=64, tag="w1_grouped")
                w1_grouped[n] = grouped
            words = w1_sb[n][:].bitcast(F32)
            pairs = w1_grouped[n][:].bitcast(F32)
            for t in (2 * half, 2 * half + 1):
                bank = transpose_words(words, BANK * t, n in SPLIT_W1)
                copy_out(n < HELPED and t % 2 == 1,
                         pairs[:, BANK * t:BANK * (t + 1)].rearrange("p (g c u) -> p g c u", g=2, u=2),
                         bank[:].rearrange("p (g u c) -> p g c u", g=2, u=2))
            if n == 0:
                spread_bb(4 + 2 * half, half == 0)
            if n == 0:
                quantise_w1(n, 2 * half, 2 * half + 2)

        def quantise_w1(n, first=0, last=TILES):
            if first == 0:
                codes = work.tile([P, K1], U32, align_bytes=64, tag="w1_codes")
                scales = work.tile([P, K1], U8, align_bytes=64, tag="w1_scales")
                w1_codes[n] = codes
                w1_scales[n] = scales
            width = K1 // TILES
            cols = slice(first * width, last * width)
            nc.vector.quantize_mx(out=w1_codes[n][:, cols].bitcast(FP8X4), scales=w1_scales[n][:, cols],
                                  in_=w1_grouped[n][:, first * K1:last * K1])

        def transpose_wb(n):
            grouped = work.tile([P, TILES * CHUNK], BF16, align_bytes=64, tag="wb_grouped")
            wb_grouped[n] = grouped
            words = wb_sb[n][:].bitcast(F32)
            pairs = grouped[:].bitcast(F32).rearrange("p (c hi lu) -> p c hi lu", hi=2, lu=4)
            for hi in range(2):
                bank = transpose_words(words, BANK * hi, n in SPLIT_WB)
                copy_out(n < HELPED, pairs[:, :, hi, :], bank[:].rearrange("p (lu c) -> p c lu", lu=4))

        def quantise_wb(n):
            codes = slow.tile([P, CHUNK], U32, align_bytes=64, tag="wb_codes")
            scales = slow.tile([P, CHUNK], U8, align_bytes=64, tag="wb_scales")
            wb_codes[n] = codes
            wb_scales[n] = scales
            nc.vector.quantize_mx(out=codes[:].bitcast(FP8X4), scales=scales[:], in_=wb_grouped[n][:])

        def stage1(n, half):
            if half == 0:
                planes = work.tile([P, TILES * BATCH], BF16, tag="h_planes")
                h_planes[n] = planes
            for t in (2 * half, 2 * half + 1):
                acc = psum.tile([P, BATCH], F32, tag="bank")
                for g in range(2):
                    lo = (2 * t + g) * P
                    nc.tensor.matmul_mx(out=acc[:], lhsT=w1_codes[n][:, lo:lo + P].bitcast(FP8X4),
                                        lhsT_scale=w1_scales[n][:, lo:lo + P],
                                        rhs=x_codes[:, g * BATCH:(g + 1) * BATCH].bitcast(FP8X4),
                                        rhs_scale=x_scales[:, g * BATCH:(g + 1) * BATCH],
                                        start=(g == 0), stop=(g == 1))
                nc.scalar.activation(out=h_planes[n][:, t * BATCH:(t + 1) * BATCH], in_=acc[:], func=RELU,
                                     bias=b1_col[:, TILES * n + t:TILES * n + t + 1], scale=1.0)

        def regroup_h(n):
            grouped = work.tile([P, TILES * BATCH], BF16, align_bytes=64, tag="h_grouped")
            h_grouped[n] = grouped
            dst = grouped[:].rearrange("p (run i t) -> p run t i", i=4, t=TILES)
            src = h_planes[n][:].rearrange("p (t run i) -> p run t i", t=TILES, i=4)
            runs = BATCH // 4
            mine = runs if n < N_CHUNKS - 1 else 5 * runs // 8
            nc.vector.tensor_copy(out=dst[:, :mine], in_=src[:, :mine])
            if mine < runs:
                nc.scalar.copy(out=dst[:, mine:], in_=src[:, mine:])

        def quantise_h(n):
            codes = work.tile([P, BATCH], U32, align_bytes=64, tag="h_codes")
            scales = work.tile([P, BATCH], U8, align_bytes=64, tag="h_scales")
            h_codes[n] = codes
            h_scales[n] = scales
            nc.vector.quantize_mx(out=codes[:].bitcast(FP8X4), scales=scales[:], in_=h_grouped[n][:])

        def stage2(n):
            for b in range(TILES):
                acc = psum.tile([P, CHUNK], F32, tag="bank")
                products[(n, b)] = acc
                nc.tensor.matmul_mx(out=acc[:], lhsT=h_codes[n][:, b * P:(b + 1) * P].bitcast(FP8X4),
                                    lhsT_scale=h_scales[n][:, b * P:(b + 1) * P],
                                    rhs=wb_codes[n][:].bitcast(FP8X4), rhs_scale=wb_scales[n][:], start=True, stop=True)

        def pieces(n):
            whole = [(b, 0, CHUNK, RELU_BY[n][b]) for b in range(TILES)]
            if n < N_CHUNKS - 1:
                return whole
            b, lo, hi, engine = whole[-1]
            return whole[:-1] + [(b, lo, hi // 2, engine), (b, hi // 2, hi, engine)]

        def store(n, b, lo, hi):
            nc.sync.dma_start(out=out_rows[:, b, n * CHUNK + lo:n * CHUNK + hi],
                              in_=out_sb[n][:, b * CHUNK + lo:b * CHUNK + hi])

        def add_bb(n):
            result = out_pool.tile([P, TILES * CHUNK], F32, tag="out_sb")
            out_sb[n] = result
            for b, lo, hi, engine in pieces(n):
                part = result[:, b * CHUNK + lo:b * CHUNK + hi]
                nc.vector.tensor_tensor(out=part, in0=products[(n, b)][:, lo:hi],
                                        in1=bb_all[:, n * CHUNK + lo:n * CHUNK + hi], op=ADD)
                if engine == "G":
                    nc.gpsimd.tensor_scalar(out=part, in0=part, scalar1=FLOAT32_MAX, scalar2=0.0, op0=MIN, op1=MAX)
                    store(n, b, lo, hi)

        def relu_on_scalar(n):
            for b, lo, hi, engine in pieces(n):
                if engine == "S":
                    part = out_sb[n][:, b * CHUNK + lo:b * CHUNK + hi]
                    nc.scalar.activation(out=part, in_=part, func=RELU)
                    store(n, b, lo, hi)

        def relu_on_vector(n):
            for b, lo, hi, engine in pieces(n):
                if engine == "V":
                    part = out_sb[n][:, b * CHUNK + lo:b * CHUNK + hi]
                    nc.vector.tensor_scalar_max(out=part, in0=part, scalar1=0.0)
                    store(n, b, lo, hi)

        def step(stage, n, *half):
            if 0 <= n < N_CHUNKS:
                stage(n, *half)

        for n in range(-W1_AHEAD, N_CHUNKS + 1):
            tail = n + W1_AHEAD >= N_CHUNKS
            step(quantise_wb, n + 1)
            step(regroup_h, n + 1)
            step(split_w1, n + W1_AHEAD + 1)
            step(transpose_w1, n + W1_AHEAD, 0)
            step(relu_on_scalar, n - 1)
            step(stage2, n)
            if tail:
                step(relu_on_vector, n - 1)
                step(quantise_h, n + 1)
            step(add_bb, n)
            step(transpose_w1, n + W1_AHEAD, 1)
            if not tail:
                step(quantise_h, n + 1)
            step(stage1, n + STAGE1_AHEAD, 0)
            step(transpose_wb, n + WB_AHEAD)
            if n + W1_AHEAD > 0:
                step(quantise_w1, n + W1_AHEAD)
            step(stage1, n + STAGE1_AHEAD, 1)
            step(split_wb, n + WB_AHEAD + 1)
            if n + W1_AHEAD + 1 < N_CHUNKS:
                step(relu_on_vector, n)
